import numpy as np
import ml_dtypes


def mxq(x, axis, fmt="e4m3"):
    dtype, down = {"e4m3": (ml_dtypes.float8_e4m3fn, 7), "e5m2": (ml_dtypes.float8_e5m2, 14)}[fmt]
    v = np.moveaxis(np.asarray(x, np.float32).astype(ml_dtypes.bfloat16).astype(np.float64), axis, -1)
    blocks = v.reshape(v.shape[:-1] + (-1, 32))
    amax = np.abs(blocks).max(-1, keepdims=True)
    byte = np.maximum(np.where(amax > 0, np.frexp(amax)[1] - 1 + 127, 0) - down, 1)
    scale = np.exp2(byte - 127.0)
    codes = (blocks / scale).astype(np.float32).astype(dtype).astype(np.float64)
    return np.moveaxis((codes * scale).reshape(v.shape), -1, axis)


WIDE = False


def mx_kscale(k):
    if not WIDE:
        return np.ones(k)
    levels = np.array([30, -30])
    if k % 512:
        return np.exp2(np.random.permutation(np.resize(levels, k // 32))).repeat(32)
    a = np.empty((k // 512, 16))
    for p in range(k // 512):
        a[p, :8] = np.random.permutation(np.resize(levels, 8))
        for g in range(8):
            far = levels[np.abs(levels - a[p, g]) >= 10]
            a[p, g + 8] = far[np.random.randint(len(far))]
    return np.exp2(a.ravel()).repeat(32)


BF16 = ml_dtypes.bfloat16


def bf(x):
    return np.asarray(x, np.float32).astype(BF16)


def f64(x):
    return np.asarray(x).astype(np.float64)


E2M1 = np.array([0.0, 0.5, 1.0, 1.5, 2.0, 3.0, 4.0, 6.0, -0.0, -0.5, -1.0, -1.5, -2.0, -3.0, -4.0, -6.0])


def pack_weight(w, fmt):
    k, n = w.shape
    w = f64(bf(w)).reshape(k // 32, 32, n)
    amax = np.abs(w).max(1)
    if fmt == "e4m3":
        byte = np.frexp(amax)[1] - 1 + 127 - 7
    else:
        mant, ex = np.frexp(amax / 6.0)
        byte = np.where(mant > 0.5, ex, ex - 1) + 127
    byte = np.clip(np.where(amax > 0, byte, 1), 1, 254)
    scaled = (w * np.exp2(127.0 - byte)[:, None, :]).reshape(k, n).astype(np.float32)
    by_word = np.ascontiguousarray(scaled.reshape(k // 512, 128, 4, n).transpose(0, 1, 3, 2))
    if fmt == "e4m3":
        words = by_word.astype(ml_dtypes.float8_e4m3fn).view(np.uint8)
    else:
        c = by_word.astype(ml_dtypes.float4_e2m1fn).view(np.uint8) & 0xF
        words = c[..., 0::2] | (c[..., 1::2] << 4)
    return np.ascontiguousarray(words), np.ascontiguousarray(byte.astype(np.uint8).reshape(k // 512, 16, n))


def unpack_weight(words, scales, fmt):
    g, p, n, _ = words.shape
    if fmt == "e4m3":
        vals = np.ascontiguousarray(words).view(ml_dtypes.float8_e4m3fn).astype(np.float64)
    else:
        nib = np.empty((g, p, n, 4), np.uint8)
        nib[..., 0::2] = words & 0xF
        nib[..., 1::2] = words >> 4
        vals = E2M1[nib]
    vals = vals * np.repeat(np.exp2(scales.astype(np.float64) - 127.0), 8, axis=1)[..., None]
    return vals.transpose(0, 1, 3, 2).reshape(g * 512, n)

def pack4(w):
    words, scales = pack_weight(w, "e2m1")
    return words.reshape(words.shape[0], 128, -1), scales


def unpack4(words, scales):
    return unpack_weight(words.reshape(words.shape[0], 128, -1, 2), scales, "e2m1")


T, K, E, H, KVH, D = 512, 1024, 2048, 16, 4, 128
EPS = 1e-05


def rmsnorm(x, w):
    var = np.mean(np.square(x), axis=-1, keepdims=True)
    return x * (1.0 / np.sqrt(var + EPS)) * w


def setup_inputs():
    s = mx_kscale(E)
    hidden_states = bf(np.random.standard_normal((T, E)) * s)
    wq = np.random.standard_normal((H * D, E)) / np.sqrt(E) / s
    words, scales = pack4(np.ascontiguousarray(wq.T))
    q_norm_w = bf(1.5 + 0.1 * np.random.standard_normal(D))
    return {"hidden_states": hidden_states,
            "Wq_words": words,
            "Wq_scales": scales,
            "q_norm_w": q_norm_w}


def reference(hidden_states, Wq_words, Wq_scales, q_norm_w):
    q = mxq(f64(hidden_states), 1, "e5m2") @ unpack4(Wq_words, Wq_scales)
    qh = rmsnorm(q.reshape(T, H, D), f64(q_norm_w))
    return qh.transpose(1, 0, 2)

@@ -1,0 +1,202 @@
+from contextlib import ExitStack
+
+import concourse.mybir as mybir
+from concourse.masks import make_identity
+
+T, E, H, D = 512, 2048, 16, 128
+EPS = 1e-05
+FLOPS = 2 * T * E * H * D
+
+F32 = mybir.dt.float32
+BF16 = mybir.dt.bfloat16
+I32 = mybir.dt.int32
+U32 = mybir.dt.uint32
+U8 = mybir.dt.uint8
+E5M2X4 = mybir.dt.float8_e5m2_x4
+E2M1X4 = mybir.dt.float4_e2m1fn_x4
+ACT = mybir.ActivationFunctionType
+ALU = mybir.AluOpType
+
+P = 128
+PASSES = 4
+TILES = 4
+CHUNK = 512
+HEADS = CHUNK // D
+CHUNKS = H * D // CHUNK
+HALF = E // 2
+XT_BANKS = 3
+ACC_BANKS = 5
+W_LOADS = ((0, 1), (1, 2), (2, 4))
+
+
+def tile_combcrossattention_pa_kernel(tc, hidden_states, Wq_words, Wq_scales, q_norm_w, out):
+    nc = tc.nc
+    x_rows = hidden_states.rearrange("(p t) k -> p t k", t=TILES)
+    out_rows = out.rearrange("h (p t) d -> p h t d", t=TILES)
+
+    with ExitStack() as ctx:
+        keep = ctx.enter_context(tc.tile_pool(name="keep", bufs=1))
+        spill = ctx.enter_context(tc.tile_pool(name="spill", bufs=2))
+        psum = ctx.enter_context(tc.psum_pool(name="psum", bufs=1))
+        ctx.enter_context(tc.manual_schedule())
+
+        gain_row = keep.tile([P, D], BF16, name="gain_row")
+        nc.gpsimd.memset(gain_row[:], 0.0)
+        nc.scalar.dma_start(out=gain_row[0:1, :], in_=q_norm_w.unsqueeze(0))
+        ident = keep.tile([P, P], F32, name="ident")
+        make_identity(nc, ident[:])
+        ones = keep.tile([P, P], BF16, name="ones")
+        nc.scalar.activation(out=ones[:], in_=ident[:], func=ACT.Abs_reciprocal_sqrt, scale=0.0, bias=1.0)
+
+        w_words = {}
+        w_scales = {}
+        for first, last in W_LOADS:
+            width = (last - first) * CHUNK
+            w_words[first] = keep.tile([P, PASSES, 2 * width], U8, name="w_words%d" % first, align_bytes=256)
+            w_scales[first] = keep.tile([P, PASSES, width], U8, name="w_scales%d" % first, align_bytes=256)
+            nc.vector.memset(w_scales[first][:].bitcast(I32), 0)
+
+        x_raw = {}
+
+        def load_x(t):
+            for half in range(2):
+                raw = keep.tile([P, HALF], BF16, name="x_raw%d%d" % (t, half))
+                nc.sync.dma_start(out=raw[:], in_=x_rows[:, t, half * HALF : (half + 1) * HALF])
+                x_raw[t, half] = raw
+
+        def load_w(first, last, pieces):
+            cols = slice(first * CHUNK, last * CHUNK)
+            for r in range(4):
+                nc.sync.dma_start(
+                    out=w_scales[first][r:P:32, :, :].bitcast(I32),
+                    in_=Wq_scales[:, r:16:4, cols].rearrange("g q n -> q g n").bitcast(I32),
+                )
+            byte_cols = slice(2 * first * CHUNK, 2 * last * CHUNK)
+            step = PASSES // pieces
+            for g0 in range(0, PASSES, step):
+                nc.sync.dma_start(
+                    out=w_words[first][:, g0 : g0 + step, :].bitcast(I32),
+                    in_=Wq_words[g0 : g0 + step, :, byte_cols].rearrange("g p n -> p g n").bitcast(I32),
+                )
+
+        load_x(0)
+        load_x(1)
+        load_w(0, 1, 2)
+        load_x(2)
+        load_x(3)
+        load_w(1, 2, 1)
+        load_w(2, 4, 1)
+
+        grouped = {}
+        x_codes = {}
+        x_scales = {}
+
+        def turn(t, half):
+            order = 2 * t + half
+            perm = keep.tile([P, 2, 2, P], F32, name="perm%d%d" % (t, half))
+            nc.vector.tensor_copy(
+                out=perm[:],
+                in_=x_raw[t, half][:].bitcast(F32).rearrange("r (g p u) -> r g u p", g=2, u=2),
+            )
+            xt = psum.tile([P, 2, 2, P], F32, name="xt", tag="xt%d" % (order % XT_BANKS))
+            for g in range(2):
+                for u in range(2):
+                    nc.tensor.transpose(xt[:, g, u, :], perm[:, g, u, :], ident[:])
+            both = keep.tile([P, HALF], BF16, name="grouped%d%d" % (t, half), align_bytes=256)
+            nc.scalar.copy(
+                out=both[:].bitcast(F32).rearrange("p (g r u) -> p g r u", g=2, u=2),
+                in_=xt[:].rearrange("p g u r -> p g r u"),
+            )
+            grouped[t, half] = both
+
+        def quantize(t, half):
+            codes = keep.tile([P, 2 * P], U32, name="x_codes%d%d" % (t, half), align_bytes=256)
+            scales = keep.tile([P, 2 * P], U8, name="x_scales%d%d" % (t, half), align_bytes=256)
+            nc.vector.quantize_mx(out=codes[:].bitcast(E5M2X4), scales=scales[:], in_=grouped[t, half][:])
+            x_codes[t, half] = codes
+            x_scales[t, half] = scales
+
+        def prepare(tiles):
+            for t in tiles:
+                for half in range(2):
+                    turn(t, half)
+            for t in tiles:
+                for half in range(2):
+                    quantize(t, half)
+
+        groups = [(t, c * HEADS, HEADS) for c in range(CHUNKS) for t in range(TILES)]
+        groups = groups[:-1] + [(TILES - 1, H - HEADS, HEADS // 2), (TILES - 1, H - HEADS // 2, HEADS // 2)]
+        sums = {}
+        rstds = {}
+        results = {}
+
+        def multiply(n):
+            t, head, heads = groups[n]
+            chunk = head // HEADS
+            first = max(f for f, last in W_LOADS if f <= chunk)
+            c0 = head * D - first * CHUNK
+            width = heads * D
+            acc = psum.tile([P, width], F32, name="acc", tag="acc%d" % ((n + 1) % ACC_BANKS))
+            for g in range(PASSES):
+                half, tok = g // 2, slice((g % 2) * P, (g % 2 + 1) * P)
+                nc.tensor.matmul_mx(
+                    out=acc[:],
+                    lhsT=x_codes[t, half][:, tok].bitcast(E5M2X4),
+                    lhsT_scale=x_scales[t, half][:, tok],
+                    rhs=w_words[first][:, g, 2 * c0 : 2 * (c0 + width)].bitcast(E2M1X4),
+                    rhs_scale=w_scales[first][:, g, c0 : c0 + width],
+                    start=(g == 0),
+                    stop=(g == PASSES - 1),
+                )
+            sums[n] = acc
+
+        def measure(n):
+            t, head, heads = groups[n]
+            squares = spill.tile([P, heads * D], BF16, name="squares")
+            ssq = keep.tile([P, heads], F32, name="ssq%d" % n)
+            for i in range(heads):
+                cols = slice(i * D, (i + 1) * D)
+                nc.scalar.activation(
+                    out=squares[:, cols], in_=sums[n][:, cols], func=ACT.Square, accum_out=ssq[:, i : i + 1]
+                )
+            rstd = keep.tile([P, heads], F32, name="rstd%d" % n)
+            nc.scalar.activation(out=rstd[:], in_=ssq[:], func=ACT.Abs_reciprocal_sqrt, scale=1.0 / D, bias=EPS)
+            rstds[n] = rstd
+
+        def finish(n):
+            t, head, heads = groups[n]
+            alone = n >= len(groups) - 3
+            t0, tokens = (t, 1) if alone else (t - t % 2, 2)
+            if t == t0:
+                results[head, t0] = keep.tile([P, heads, tokens, D], F32, name="result%d" % n)
+            result = results[head, t0]
+            for i in range(heads):
+                nc.vector.scalar_tensor_tensor(
+                    out=result[:, i, t - t0, :],
+                    in0=sums[n][:, i * D : (i + 1) * D],
+                    scalar=rstds[n][:, i : i + 1],
+                    in1=gain[:],
+                    op0=ALU.mult,
+                    op1=ALU.mult,
+                )
+            if t == t0 + tokens - 1:
+                nc.sync.dma_start(out=out_rows[:, head : head + heads, t0 : t0 + tokens, :], in_=result[:])
+
+        prepare((0, 1))
+
+        gain_ps = psum.tile([P, D], F32, name="gain_ps", tag="acc0")
+        nc.tensor.matmul(out=gain_ps[:], lhsT=ones[:], rhs=gain_row[:], start=True, stop=True)
+        gain = keep.tile([P, D], F32, name="gain")
+        nc.scalar.copy(out=gain[:], in_=gain_ps[:])
+
+        multiply(0)
+        multiply(1)
+        measure(0)
+        prepare((2, 3))
+        finish(0)
+        measure(1)
+        finish(1)
+        for n in range(2, len(groups)):
+            multiply(n)
+            measure(n)
+            finish(n)

@@ -116,10 +116,17 @@ def tile_combcrossattention_pa_kernel(tc, hidden_states, Wq_words, Wq_scales, q_
             x_codes[t, half] = codes
             x_scales[t, half] = scales
 
+        def warm_up(count):
+            unread = psum.tile([P, P], F32, name="unread", tag="acc%d" % (ACC_BANKS - 1))
+            for i in range(count):
+                nc.tensor.matmul(out=unread[:], lhsT=ident[:], rhs=ident[:], start=True, stop=True)
+
         def prepare(tiles):
             for t in tiles:
                 for half in range(2):
                     turn(t, half)
+                if t < 2:
+                    warm_up(1)
             for t in tiles:
                 for half in range(2):
                     quantize(t, half)
@@ -182,6 +189,7 @@ def tile_combcrossattention_pa_kernel(tc, hidden_states, Wq_words, Wq_scales, q_
             if t == t0 + tokens - 1:
                 nc.sync.dma_start(out=out_rows[:, head : head + heads, t0 : t0 + tokens, :], in_=result[:])
 
+        warm_up(3)
         prepare((0, 1))
 
         gain_ps = psum.tile([P, D], F32, name="gain_ps", tag="acc0")

@@ -24,8 +24,7 @@ CHUNK = 512
 HEADS = CHUNK // D
 CHUNKS = H * D // CHUNK
 HALF = E // 2
-XT_BANKS = 3
-ACC_BANKS = 5
+BANKS = 8
 W_LOADS = ((0, 1), (1, 2), (2, 4))
 
 
@@ -82,30 +81,44 @@ def tile_combcrossattention_pa_kernel(tc, hidden_states, Wq_words, Wq_scales, q_
         load_x(0)
         load_x(1)
         load_w(0, 1, 2)
+        load_w(1, 2, 2)
         load_x(2)
         load_x(3)
-        load_w(1, 2, 1)
-        load_w(2, 4, 1)
+        load_w(2, 4, 2)
 
+        taken = []
+
+        def bank(shape, name):
+            taken.append(name)
+            return psum.tile(shape, F32, name=name, tag="bank%d" % ((len(taken) - 1) % BANKS))
+
+        perms = {}
+        turned = {}
         grouped = {}
         x_codes = {}
         x_scales = {}
 
-        def turn(t, half):
-            order = 2 * t + half
+        def reorder(t, half):
             perm = keep.tile([P, 2, 2, P], F32, name="perm%d%d" % (t, half))
             nc.vector.tensor_copy(
                 out=perm[:],
                 in_=x_raw[t, half][:].bitcast(F32).rearrange("r (g p u) -> r g u p", g=2, u=2),
             )
-            xt = psum.tile([P, 2, 2, P], F32, name="xt", tag="xt%d" % (order % XT_BANKS))
+            perms[t, half] = perm
+
+        def turn(t, half):
+            xt = bank([P, 2, 2, P], "xt")
             for g in range(2):
                 for u in range(2):
-                    nc.tensor.transpose(xt[:, g, u, :], perm[:, g, u, :], ident[:])
+                    nc.tensor.transpose(xt[:, g, u, :], perms[t, half][:, g, u, :], ident[:])
+            turned[t, half] = xt
+
+        def interleave(t, half):
             both = keep.tile([P, HALF], BF16, name="grouped%d%d" % (t, half), align_bytes=256)
-            nc.scalar.copy(
+            copy = nc.vector.tensor_copy if (t, half) == (TILES - 1, 0) else nc.scalar.copy
+            copy(
                 out=both[:].bitcast(F32).rearrange("p (g r u) -> p g r u", g=2, u=2),
-                in_=xt[:].rearrange("p g u r -> p g r u"),
+                in_=turned[t, half][:].rearrange("p g u r -> p g r u"),
             )
             grouped[t, half] = both
 
@@ -117,22 +130,17 @@ def tile_combcrossattention_pa_kernel(tc, hidden_states, Wq_words, Wq_scales, q_
             x_scales[t, half] = scales
 
         def warm_up(count):
-            unread = psum.tile([P, P], F32, name="unread", tag="acc%d" % (ACC_BANKS - 1))
+            unread = psum.tile([P, P], F32, name="unread", tag="bank%d" % (BANKS - 1))
             for i in range(count):
                 nc.tensor.matmul(out=unread[:], lhsT=ident[:], rhs=ident[:], start=True, stop=True)
 
-        def prepare(tiles):
-            for t in tiles:
-                for half in range(2):
-                    turn(t, half)
-                if t < 2:
-                    warm_up(1)
-            for t in tiles:
-                for half in range(2):
-                    quantize(t, half)
-
-        groups = [(t, c * HEADS, HEADS) for c in range(CHUNKS) for t in range(TILES)]
-        groups = groups[:-1] + [(TILES - 1, H - HEADS, HEADS // 2), (TILES - 1, H - HEADS // 2, HEADS // 2)]
+        groups = [(t, c * HEADS, HEADS) for c in range(2) for t in range(2)]
+        groups += [(t, c * HEADS, HEADS) for t in range(2, TILES) for c in range(2)]
+        groups += [(t, 2 * HEADS, HEADS) for t in range(TILES)]
+        groups += [(t, head, 2) for t0 in (0, 2) for head in (H - 4, H - 2) for t in (t0, t0 + 1)][:-1]
+        paired = len(groups) - 1
+        groups += [(TILES - 1, H - 2, 1), (TILES - 1, H - 1, 1)]
+        ssqs = {}
         sums = {}
         rstds = {}
         results = {}
@@ -143,7 +151,7 @@ def tile_combcrossattention_pa_kernel(tc, hidden_states, Wq_words, Wq_scales, q_
             first = max(f for f, last in W_LOADS if f <= chunk)
             c0 = head * D - first * CHUNK
             width = heads * D
-            acc = psum.tile([P, width], F32, name="acc", tag="acc%d" % ((n + 1) % ACC_BANKS))
+            acc = bank([P, width], "acc")
             for g in range(PASSES):
                 half, tok = g // 2, slice((g % 2) * P, (g % 2 + 1) * P)
                 nc.tensor.matmul_mx(
@@ -157,23 +165,29 @@ def tile_combcrossattention_pa_kernel(tc, hidden_states, Wq_words, Wq_scales, q_
                 )
             sums[n] = acc
 
-        def measure(n):
+        def square(n, first_head, last_head):
             t, head, heads = groups[n]
-            squares = spill.tile([P, heads * D], BF16, name="squares")
-            ssq = keep.tile([P, heads], F32, name="ssq%d" % n)
-            for i in range(heads):
+            if first_head == 0:
+                squares = spill.tile([P, heads * D], BF16, name="squares")
+                ssq = keep.tile([P, heads], F32, name="ssq%d" % n)
+                ssqs[n] = (squares, ssq)
+            squares, ssq = ssqs[n]
+            for i in range(first_head, last_head):
                 cols = slice(i * D, (i + 1) * D)
                 nc.scalar.activation(
                     out=squares[:, cols], in_=sums[n][:, cols], func=ACT.Square, accum_out=ssq[:, i : i + 1]
                 )
-            rstd = keep.tile([P, heads], F32, name="rstd%d" % n)
-            nc.scalar.activation(out=rstd[:], in_=ssq[:], func=ACT.Abs_reciprocal_sqrt, scale=1.0 / D, bias=EPS)
+
+        def root(n):
+            rstd = keep.tile([P, groups[n][2]], F32, name="rstd%d" % n)
+            nc.scalar.activation(
+                out=rstd[:], in_=ssqs[n][1][:], func=ACT.Abs_reciprocal_sqrt, scale=1.0 / D, bias=EPS
+            )
             rstds[n] = rstd
 
         def finish(n):
             t, head, heads = groups[n]
-            alone = n >= len(groups) - 3
-            t0, tokens = (t, 1) if alone else (t - t % 2, 2)
+            t0, tokens = (t - t % 2, 2) if n < paired else (t, 1)
             if t == t0:
                 results[head, t0] = keep.tile([P, heads, tokens, D], F32, name="result%d" % n)
             result = results[head, t0]
@@ -190,21 +204,66 @@ def tile_combcrossattention_pa_kernel(tc, hidden_states, Wq_words, Wq_scales, q_
                 nc.sync.dma_start(out=out_rows[:, head : head + heads, t0 : t0 + tokens, :], in_=result[:])
 
         warm_up(3)
-        prepare((0, 1))
-
-        gain_ps = psum.tile([P, D], F32, name="gain_ps", tag="acc0")
+        for half in range(2):
+            reorder(0, half)
+            turn(0, half)
+            interleave(0, half)
+        warm_up(1)
+        gain_ps = bank([P, D], "gain_ps")
         nc.tensor.matmul(out=gain_ps[:], lhsT=ones[:], rhs=gain_row[:], start=True, stop=True)
+        for half in range(2):
+            reorder(1, half)
+            turn(1, half)
+            interleave(1, half)
+        warm_up(1)
         gain = keep.tile([P, D], F32, name="gain")
         nc.scalar.copy(out=gain[:], in_=gain_ps[:])
+        for t in range(2):
+            for half in range(2):
+                quantize(t, half)
+
+        def measure(n):
+            square(n, 0, groups[n][2])
+            root(n)
+
+        def step(n):
+            multiply(n)
+            square(n, 0, 1)
+            root(n - 1)
+            square(n, 1, groups[n][2])
 
         multiply(0)
-        multiply(1)
         measure(0)
-        prepare((2, 3))
         finish(0)
+        multiply(1)
         measure(1)
+        reorder(2, 0)
+        reorder(2, 1)
         finish(1)
-        for n in range(2, len(groups)):
-            multiply(n)
-            measure(n)
-            finish(n)
+        multiply(2)
+        measure(2)
+        reorder(3, 0)
+        finish(2)
+        reorder(3, 1)
+        multiply(3)
+        for t in range(2, TILES):
+            for half in range(2):
+                turn(t, half)
+        for half in range(2):
+            interleave(2, half)
+        for half in range(2):
+            quantize(2, half)
+        interleave(3, 0)
+        square(3, 0, HEADS)
+        interleave(3, 1)
+        root(3)
+        for half in range(2):
+            quantize(3, half)
+        finish(3)
+        multiply(4)
+        square(4, 0, HEADS)
+        for n in range(5, len(groups)):
+            step(n)
+            finish(n - 1)
+        root(len(groups) - 1)
+        finish(len(groups) - 1)

@@ -215,7 +215,7 @@ def tile_combcrossattention_pa_kernel(tc, hidden_states, Wq_words, Wq_scales, q_
             reorder(1, half)
             turn(1, half)
             interleave(1, half)
-        warm_up(1)
+        warm_up(2)
         gain = keep.tile([P, D], F32, name="gain")
         nc.scalar.copy(out=gain[:], in_=gain_ps[:])
         for t in range(2):

from contextlib import ExitStack

import concourse.mybir as mybir
from concourse.masks import make_identity

T, E, H, D = 512, 2048, 16, 128
EPS = 1e-05
FLOPS = 2 * T * E * H * D

F32 = mybir.dt.float32
BF16 = mybir.dt.bfloat16
I32 = mybir.dt.int32
U32 = mybir.dt.uint32
U8 = mybir.dt.uint8
E5M2X4 = mybir.dt.float8_e5m2_x4
E2M1X4 = mybir.dt.float4_e2m1fn_x4
ACT = mybir.ActivationFunctionType
ALU = mybir.AluOpType

P = 128
PASSES = 4
TILES = 4
CHUNK = 512
HEADS = CHUNK // D
CHUNKS = H * D // CHUNK
HALF = E // 2
BANKS = 8
W_LOADS = ((0, 1), (1, 2), (2, 4))


def tile_combcrossattention_pa_kernel(tc, hidden_states, Wq_words, Wq_scales, q_norm_w, out):
    nc = tc.nc
    x_rows = hidden_states.rearrange("(p t) k -> p t k", t=TILES)
    out_rows = out.rearrange("h (p t) d -> p h t d", t=TILES)

    with ExitStack() as ctx:
        keep = ctx.enter_context(tc.tile_pool(name="keep", bufs=1))
        spill = ctx.enter_context(tc.tile_pool(name="spill", bufs=2))
        psum = ctx.enter_context(tc.psum_pool(name="psum", bufs=1))
        ctx.enter_context(tc.manual_schedule())

        gain_row = keep.tile([P, D], BF16, name="gain_row")
        nc.gpsimd.memset(gain_row[:], 0.0)
        nc.scalar.dma_start(out=gain_row[0:1, :], in_=q_norm_w.unsqueeze(0))
        ident = keep.tile([P, P], F32, name="ident")
        make_identity(nc, ident[:])
        ones = keep.tile([P, P], BF16, name="ones")
        nc.scalar.activation(out=ones[:], in_=ident[:], func=ACT.Abs_reciprocal_sqrt, scale=0.0, bias=1.0)

        w_words = {}
        w_scales = {}
        for first, last in W_LOADS:
            width = (last - first) * CHUNK
            w_words[first] = keep.tile([P, PASSES, 2 * width], U8, name="w_words%d" % first, align_bytes=256)
            w_scales[first] = keep.tile([P, PASSES, width], U8, name="w_scales%d" % first, align_bytes=256)
            nc.vector.memset(w_scales[first][:].bitcast(I32), 0)

        x_raw = {}

        def load_x(t):
            for half in range(2):
                raw = keep.tile([P, HALF], BF16, name="x_raw%d%d" % (t, half))
                nc.sync.dma_start(out=raw[:], in_=x_rows[:, t, half * HALF : (half + 1) * HALF])
                x_raw[t, half] = raw

        def load_w(first, last, pieces):
            cols = slice(first * CHUNK, last * CHUNK)
            for r in range(4):
                nc.sync.dma_start(
                    out=w_scales[first][r:P:32, :, :].bitcast(I32),
                    in_=Wq_scales[:, r:16:4, cols].rearrange("g q n -> q g n").bitcast(I32),
                )
            byte_cols = slice(2 * first * CHUNK, 2 * last * CHUNK)
            step = PASSES // pieces
            for g0 in range(0, PASSES, step):
                nc.sync.dma_start(
                    out=w_words[first][:, g0 : g0 + step, :].bitcast(I32),
                    in_=Wq_words[g0 : g0 + step, :, byte_cols].rearrange("g p n -> p g n").bitcast(I32),
                )

        load_x(0)
        load_x(1)
        load_w(0, 1, 2)
        load_w(1, 2, 2)
        load_x(2)
        load_x(3)
        load_w(2, 4, 2)

        taken = []

        def bank(shape, name):
            taken.append(name)
            return psum.tile(shape, F32, name=name, tag="bank%d" % ((len(taken) - 1) % BANKS))

        perms = {}
        turned = {}
        grouped = {}
        x_codes = {}
        x_scales = {}

        def reorder(t, half):
            perm = keep.tile([P, 2, 2, P], F32, name="perm%d%d" % (t, half))
            nc.vector.tensor_copy(
                out=perm[:],
                in_=x_raw[t, half][:].bitcast(F32).rearrange("r (g p u) -> r g u p", g=2, u=2),
            )
            perms[t, half] = perm

        def turn(t, half):
            xt = bank([P, 2, 2, P], "xt")
            for g in range(2):
                for u in range(2):
                    nc.tensor.transpose(xt[:, g, u, :], perms[t, half][:, g, u, :], ident[:])
            turned[t, half] = xt

        def interleave(t, half):
            both = keep.tile([P, HALF], BF16, name="grouped%d%d" % (t, half), align_bytes=256)
            copy = nc.vector.tensor_copy if (t, half) == (TILES - 1, 0) else nc.scalar.copy
            copy(
                out=both[:].bitcast(F32).rearrange("p (g r u) -> p g r u", g=2, u=2),
                in_=turned[t, half][:].rearrange("p g u r -> p g r u"),
            )
            grouped[t, half] = both

        def quantize(t, half):
            codes = keep.tile([P, 2 * P], U32, name="x_codes%d%d" % (t, half), align_bytes=256)
            scales = keep.tile([P, 2 * P], U8, name="x_scales%d%d" % (t, half), align_bytes=256)
            nc.vector.quantize_mx(out=codes[:].bitcast(E5M2X4), scales=scales[:], in_=grouped[t, half][:])
            x_codes[t, half] = codes
            x_scales[t, half] = scales

        def warm_up(count):
            unread = psum.tile([P, P], F32, name="unread", tag="bank%d" % (BANKS - 1))
            for i in range(count):
                nc.tensor.matmul(out=unread[:], lhsT=ident[:], rhs=ident[:], start=True, stop=True)

        groups = [(t, c * HEADS, HEADS) for c in range(2) for t in range(2)]
        groups += [(t, c * HEADS, HEADS) for t in range(2, TILES) for c in range(2)]
        groups += [(t, 2 * HEADS, HEADS) for t in range(TILES)]
        groups += [(t, head, 2) for t0 in (0, 2) for head in (H - 4, H - 2) for t in (t0, t0 + 1)][:-1]
        paired = len(groups) - 1
        groups += [(TILES - 1, H - 2, 1), (TILES - 1, H - 1, 1)]
        ssqs = {}
        sums = {}
        rstds = {}
        results = {}

        def multiply(n):
            t, head, heads = groups[n]
            chunk = head // HEADS
            first = max(f for f, last in W_LOADS if f <= chunk)
            c0 = head * D - first * CHUNK
            width = heads * D
            acc = bank([P, width], "acc")
            for g in range(PASSES):
                half, tok = g // 2, slice((g % 2) * P, (g % 2 + 1) * P)
                nc.tensor.matmul_mx(
                    out=acc[:],
                    lhsT=x_codes[t, half][:, tok].bitcast(E5M2X4),
                    lhsT_scale=x_scales[t, half][:, tok],
                    rhs=w_words[first][:, g, 2 * c0 : 2 * (c0 + width)].bitcast(E2M1X4),
                    rhs_scale=w_scales[first][:, g, c0 : c0 + width],
                    start=(g == 0),
                    stop=(g == PASSES - 1),
                )
            sums[n] = acc

        def square(n, first_head, last_head):
            t, head, heads = groups[n]
            if first_head == 0:
                squares = spill.tile([P, heads * D], BF16, name="squares")
                ssq = keep.tile([P, heads], F32, name="ssq%d" % n)
                ssqs[n] = (squares, ssq)
            squares, ssq = ssqs[n]
            for i in range(first_head, last_head):
                cols = slice(i * D, (i + 1) * D)
                nc.scalar.activation(
                    out=squares[:, cols], in_=sums[n][:, cols], func=ACT.Square, accum_out=ssq[:, i : i + 1]
                )

        def root(n):
            rstd = keep.tile([P, groups[n][2]], F32, name="rstd%d" % n)
            nc.scalar.activation(
                out=rstd[:], in_=ssqs[n][1][:], func=ACT.Abs_reciprocal_sqrt, scale=1.0 / D, bias=EPS
            )
            rstds[n] = rstd

        def finish(n):
            t, head, heads = groups[n]
            t0, tokens = (t - t % 2, 2) if n < paired else (t, 1)
            if t == t0:
                results[head, t0] = keep.tile([P, heads, tokens, D], F32, name="result%d" % n)
            result = results[head, t0]
            for i in range(heads):
                nc.vector.scalar_tensor_tensor(
                    out=result[:, i, t - t0, :],
                    in0=sums[n][:, i * D : (i + 1) * D],
                    scalar=rstds[n][:, i : i + 1],
                    in1=gain[:],
                    op0=ALU.mult,
                    op1=ALU.mult,
                )
            if t == t0 + tokens - 1:
                nc.sync.dma_start(out=out_rows[:, head : head + heads, t0 : t0 + tokens, :], in_=result[:])

        warm_up(3)
        for half in range(2):
            reorder(0, half)
            turn(0, half)
            interleave(0, half)
        warm_up(1)
        gain_ps = bank([P, D], "gain_ps")
        nc.tensor.matmul(out=gain_ps[:], lhsT=ones[:], rhs=gain_row[:], start=True, stop=True)
        for half in range(2):
            reorder(1, half)
            turn(1, half)
            interleave(1, half)
        warm_up(2)
        gain = keep.tile([P, D], F32, name="gain")
        nc.scalar.copy(out=gain[:], in_=gain_ps[:])
        for t in range(2):
            for half in range(2):
                quantize(t, half)

        def measure(n):
            square(n, 0, groups[n][2])
            root(n)

        def step(n):
            multiply(n)
            square(n, 0, 1)
            root(n - 1)
            square(n, 1, groups[n][2])

        multiply(0)
        measure(0)
        finish(0)
        multiply(1)
        measure(1)
        reorder(2, 0)
        reorder(2, 1)
        finish(1)
        multiply(2)
        measure(2)
        reorder(3, 0)
        finish(2)
        reorder(3, 1)
        multiply(3)
        for t in range(2, TILES):
            for half in range(2):
                turn(t, half)
        for half in range(2):
            interleave(2, half)
        for half in range(2):
            quantize(2, half)
        interleave(3, 0)
        square(3, 0, HEADS)
        interleave(3, 1)
        root(3)
        for half in range(2):
            quantize(3, half)
        finish(3)
        multiply(4)
        square(4, 0, HEADS)
        for n in range(5, len(groups)):
            step(n)
            finish(n - 1)
        root(len(groups) - 1)
        finish(len(groups) - 1)
